import numpy as np
import ml_dtypes


def mxq(x, axis, fmt="e4m3"):
    dtype, down = {"e4m3": (ml_dtypes.float8_e4m3fn, 7), "e5m2": (ml_dtypes.float8_e5m2, 14)}[fmt]
    v = np.moveaxis(np.asarray(x, np.float32).astype(ml_dtypes.bfloat16).astype(np.float64), axis, -1)
    blocks = v.reshape(v.shape[:-1] + (-1, 32))
    amax = np.abs(blocks).max(-1, keepdims=True)
    byte = np.maximum(np.where(amax > 0, np.frexp(amax)[1] - 1 + 127, 0) - down, 1)
    scale = np.exp2(byte - 127.0)
    codes = (blocks / scale).astype(np.float32).astype(dtype).astype(np.float64)
    return np.moveaxis((codes * scale).reshape(v.shape), -1, axis)


WIDE = False


def mx_kscale(k):
    if not WIDE:
        return np.ones(k)
    levels = np.array([10, -10, 5, -5, 0])
    a = np.random.permutation(np.resize(levels, k // 512 * 4)).reshape(k // 512, 4)
    idx = np.arange(k)
    return np.exp2(a[idx // 512, idx % 128 // 32])


BF16 = ml_dtypes.bfloat16


def bf(x):
    return np.asarray(x, np.float32).astype(BF16)


def f64(x):
    return np.asarray(x).astype(np.float64)


B, L, D, F, K = 128, 8, 128, 1024, 16
EPS = 1e-12


def silu(v):
    return v / (1.0 + np.exp(-v))


def l2norm(t, axis):
    n = np.sqrt((t * t).sum(axis=axis, keepdims=True))
    return t / np.maximum(n, EPS)


def mix_draw(rows, cols):
    return np.random.standard_normal((L, rows, cols)) * np.sqrt(np.e / K) * np.exp(0.5 * np.random.standard_normal((L, 1, cols)))


def hidden_draw():
    return silu(3.0 * np.random.standard_normal((B, L, F))) * np.random.standard_normal((B, L, F)) * 3.0 / np.sqrt(D)


def setup_inputs():
    t = mx_kscale(F)
    g = np.sqrt(np.mean(1.0 / t**2))
    return {"h": bf(hidden_draw() * t * g),
            "w_down_mix": bf(mix_draw(F, D) / t[:, None])}


def reference(h, w_down_mix):
    wd = l2norm(f64(w_down_mix), 1)
    y = mxq(f64(h).transpose(1, 0, 2), 2, "e4m3") @ mxq(wd, 1, "e4m3")
    return l2norm(y, -1).transpose(1, 0, 2)

@@ -1,0 +1,173 @@
+import concourse.mybir as mybir
+from concourse.masks import make_identity
+
+F32 = mybir.dt.float32
+BF16 = mybir.dt.bfloat16
+U32 = mybir.dt.uint32
+U8 = mybir.dt.uint8
+FP8X4 = mybir.dt.float8_e4m3fn_x4
+ACT = mybir.ActivationFunctionType
+ALU = mybir.AluOpType
+
+P = 128
+B, L, F, D = 128, 8, 1024, 128
+PACK = 4
+PASSES = F // (P * PACK)
+ROWS = F // P
+HALVES = 2
+PAIR = 2
+BANK_TOKENS = 4
+EPS = 1e-12
+
+FLOPS = 2 * B * L * F * D
+
+
+def tile_npertokenswishglu_basis_pb_s_kernel(tc, h, w_down_mix, out):
+    nc = tc.nc
+    with tc.tile_pool(name="keep", bufs=1) as keep, tc.psum_pool(
+        name="wt_psum", bufs=2
+    ) as wt_psum, tc.psum_pool(name="ht_psum", bufs=2) as ht_psum, tc.psum_pool(
+        name="scale_psum", bufs=2
+    ) as scale_psum, tc.psum_pool(name="y_psum", bufs=2) as y_psum:
+        w_sb = keep.tile([P, L, ROWS, D], BF16)
+        h_sb = keep.tile([P, L, F], BF16)
+        for l in range(L):
+            nc.sync.dma_start(
+                out=w_sb[:, l].rearrange("p (s e) j -> p s (e j)", e=2),
+                in_=w_down_mix[l].rearrange("(s p e) j -> p s (e j)", p=P, e=2),
+            )
+            nc.sync.dma_start(out=h_sb[:, l, :], in_=h[:, l, :])
+        h_words = h_sb[:].bitcast(F32)
+
+        ident_bf = keep.tile([P, P], BF16)
+        make_identity(nc, ident_bf[:])
+        ident_f32 = keep.tile([P, P], F32)
+        make_identity(nc, ident_f32[:])
+
+        one = keep.tile([P, 1], F32)
+        nc.vector.memset(one[:], 1.0)
+        warm = keep.tile([P, 1], F32)
+        nc.scalar.activation(out=warm[:], in_=one[:], func=ACT.Sqrt)
+
+        w_squares = keep.tile([P, L, ROWS, P], BF16)
+        w_sumsq = keep.tile([P, L], F32)
+        w_sumsq_floor = keep.tile([P, L], F32)
+        w_inv_sumsq = keep.tile([P, L], F32)
+        w_scale_rep = keep.tile([P, L, P], F32)
+        nd_grouped = keep.tile([P, L, PASSES, D, PACK], BF16, align_bytes=64)
+        nd_codes = keep.tile([P, L, PASSES, D], U32, align_bytes=64)
+        nd_scales = keep.tile([P, L, PASSES, D], U8, align_bytes=64)
+        h_grouped = keep.tile([P, L, PASSES, B, PACK], BF16, align_bytes=64)
+        h_codes = keep.tile([P, L, PASSES, B], U32, align_bytes=64)
+        h_scales = keep.tile([P, L, PASSES, B], U8, align_bytes=64)
+        y_squares = keep.tile([P, L, D], F32)
+        y_sumsq = keep.tile([P, L], F32)
+        y_sumsq_floor = keep.tile([P, L], F32)
+        y_inv_sumsq = keep.tile([P, L], F32)
+        y_scale = keep.tile([P, L], F32)
+        out_sb = keep.tile([P, L, D], F32)
+
+        def weight_norm(l):
+            wT = wt_psum.tile([P, ROWS, P], BF16)
+            for r in range(ROWS):
+                nc.tensor.transpose(wT[:, r, :], w_sb[:, l, r, :], ident_bf[:])
+            nc.scalar.activation(
+                out=w_squares[:, l], in_=wT[:], func=ACT.Square, accum_out=w_sumsq[:, l : l + 1]
+            )
+
+        def quantise_h(l):
+            hT = ht_psum.tile([P, PASSES, HALVES, B], F32)
+            for g in range(PASSES):
+                for u in range(HALVES):
+                    first = (g * HALVES + u) * P
+                    nc.tensor.transpose(
+                        hT[:, g, u, :], h_words[:, l, first : first + P], ident_f32[:]
+                    )
+            nc.scalar.copy(
+                out=h_grouped[:, l].bitcast(F32), in_=hT[:].rearrange("p g u b -> p g b u")
+            )
+            nc.vector.quantize_mx(
+                out=h_codes[:, l].rearrange("p g b -> p (g b)").bitcast(FP8X4),
+                scales=h_scales[:, l].rearrange("p g b -> p (g b)"),
+                in_=h_grouped[:, l].rearrange("p g b t -> p (g b t)"),
+            )
+
+        def spread_scales(first):
+            ls = slice(first, first + PAIR)
+            nc.vector.tensor_scalar_max(
+                out=w_sumsq_floor[:, ls], in0=w_sumsq[:, ls], scalar1=EPS * EPS
+            )
+            nc.vector.reciprocal(out=w_inv_sumsq[:, ls], in_=w_sumsq_floor[:, ls])
+            nc.scalar.activation(
+                out=w_scale_rep[:, ls, :],
+                in_=w_inv_sumsq[:, ls].unsqueeze(2).to_broadcast([P, PAIR, P]),
+                func=ACT.Sqrt,
+            )
+            w_scale = scale_psum.tile([P, PAIR, D], F32)
+            for i in range(PAIR):
+                nc.tensor.transpose(w_scale[:, i, :], w_scale_rep[:, first + i, :], ident_f32[:])
+            return w_scale
+
+        def quantise_nd(l, w_scale_l):
+            nc.vector.tensor_tensor(
+                out=nd_grouped[:, l],
+                in0=w_sb[:, l].rearrange("p (g t) j -> p g j t", t=PACK),
+                in1=w_scale_l.unsqueeze(1).unsqueeze(3).to_broadcast([P, PASSES, D, PACK]),
+                op=ALU.mult,
+            )
+            nc.vector.quantize_mx(
+                out=nd_codes[:, l].rearrange("p g j -> p (g j)").bitcast(FP8X4),
+                scales=nd_scales[:, l].rearrange("p g j -> p (g j)"),
+                in_=nd_grouped[:, l].rearrange("p g j t -> p (g j t)"),
+            )
+
+        def multiply(l, y):
+            for g in range(PASSES):
+                nc.tensor.matmul_mx(
+                    out=y[:, l % BANK_TOKENS, :],
+                    lhsT=h_codes[:, l, g, :].bitcast(FP8X4),
+                    lhsT_scale=h_scales[:, l, g, :],
+                    rhs=nd_codes[:, l, g, :].bitcast(FP8X4),
+                    rhs_scale=nd_scales[:, l, g, :],
+                    start=(g == 0),
+                    stop=(g == PASSES - 1),
+                )
+            nc.scalar.activation(
+                out=y_squares[:, l, :],
+                in_=y[:, l % BANK_TOKENS, :],
+                func=ACT.Square,
+                accum_out=y_sumsq[:, l : l + 1],
+            )
+
+        def normalise_and_store(first, y):
+            ls = slice(first, first + BANK_TOKENS)
+            nc.vector.tensor_scalar_max(
+                out=y_sumsq_floor[:, ls], in0=y_sumsq[:, ls], scalar1=EPS * EPS
+            )
+            nc.vector.reciprocal(out=y_inv_sumsq[:, ls], in_=y_sumsq_floor[:, ls])
+            nc.scalar.activation(out=y_scale[:, ls], in_=y_inv_sumsq[:, ls], func=ACT.Sqrt)
+            nc.vector.tensor_tensor(
+                out=out_sb[:, ls, :],
+                in0=y[:],
+                in1=y_scale[:, ls].unsqueeze(2).to_broadcast([P, BANK_TOKENS, D]),
+                op=ALU.mult,
+            )
+            nc.sync.dma_start(out=out[:, ls, :], in_=out_sb[:, ls, :])
+
+        y = None
+        for first in range(0, L + PAIR, PAIR):
+            if first < L:
+                for l in range(first, first + PAIR):
+                    weight_norm(l)
+                    quantise_h(l)
+            if first >= PAIR:
+                done = first - PAIR
+                w_scale = spread_scales(done)
+                if done % BANK_TOKENS == 0:
+                    y = y_psum.tile([P, BANK_TOKENS, D], F32)
+                for i in range(PAIR):
+                    quantise_nd(done + i, w_scale[:, i, :])
+                for i in range(PAIR):
+                    multiply(done + i, y)
+                if (done + PAIR) % BANK_TOKENS == 0:
+                    normalise_and_store(done + PAIR - BANK_TOKENS, y)

@@ -15,11 +15,13 @@ PACK = 4
 PASSES = F // (P * PACK)
 ROWS = F // P
 HALVES = 2
-PAIR = 2
-BANK_TOKENS = 4
 EPS = 1e-12
 
 FLOPS = 2 * B * L * F * D
+
+H_COPIES_ON_VECTOR = 2
+STORE_TOKENS = 2
+BANK_TOKENS = 4
 
 
 def tile_npertokenswishglu_basis_pb_s_kernel(tc, h, w_down_mix, out):
@@ -28,7 +30,7 @@ def tile_npertokenswishglu_basis_pb_s_kernel(tc, h, w_down_mix, out):
         name="wt_psum", bufs=2
     ) as wt_psum, tc.psum_pool(name="ht_psum", bufs=2) as ht_psum, tc.psum_pool(
         name="scale_psum", bufs=2
-    ) as scale_psum, tc.psum_pool(name="y_psum", bufs=2) as y_psum:
+    ) as scale_psum, tc.psum_pool(name="y_psum", bufs=2) as y_psum, tc.manual_schedule():
         w_sb = keep.tile([P, L, ROWS, D], BF16)
         h_sb = keep.tile([P, L, F], BF16)
         for l in range(L):
@@ -47,13 +49,11 @@ def tile_npertokenswishglu_basis_pb_s_kernel(tc, h, w_down_mix, out):
         one = keep.tile([P, 1], F32)
         nc.vector.memset(one[:], 1.0)
         warm = keep.tile([P, 1], F32)
-        nc.scalar.activation(out=warm[:], in_=one[:], func=ACT.Sqrt)
+        nc.scalar.activation(out=warm[:], in_=one[:], func=ACT.Abs_reciprocal_sqrt)
 
         w_squares = keep.tile([P, L, ROWS, P], BF16)
         w_sumsq = keep.tile([P, L], F32)
-        w_sumsq_floor = keep.tile([P, L], F32)
-        w_inv_sumsq = keep.tile([P, L], F32)
-        w_scale_rep = keep.tile([P, L, P], F32)
+        w_rsqrt = keep.tile([P, L], F32)
         nd_grouped = keep.tile([P, L, PASSES, D, PACK], BF16, align_bytes=64)
         nd_codes = keep.tile([P, L, PASSES, D], U32, align_bytes=64)
         nd_scales = keep.tile([P, L, PASSES, D], U8, align_bytes=64)
@@ -62,20 +62,13 @@ def tile_npertokenswishglu_basis_pb_s_kernel(tc, h, w_down_mix, out):
         h_scales = keep.tile([P, L, PASSES, B], U8, align_bytes=64)
         y_squares = keep.tile([P, L, D], F32)
         y_sumsq = keep.tile([P, L], F32)
-        y_sumsq_floor = keep.tile([P, L], F32)
-        y_inv_sumsq = keep.tile([P, L], F32)
-        y_scale = keep.tile([P, L], F32)
+        y_rsqrt = keep.tile([P, L], F32)
         out_sb = keep.tile([P, L, D], F32)
+        w_rsqrt_spread = {}
+        y = {}
 
-        def weight_norm(l):
-            wT = wt_psum.tile([P, ROWS, P], BF16)
-            for r in range(ROWS):
-                nc.tensor.transpose(wT[:, r, :], w_sb[:, l, r, :], ident_bf[:])
-            nc.scalar.activation(
-                out=w_squares[:, l], in_=wT[:], func=ACT.Square, accum_out=w_sumsq[:, l : l + 1]
-            )
 
-        def quantise_h(l):
+        def transpose_h(l):
             hT = ht_psum.tile([P, PASSES, HALVES, B], F32)
             for g in range(PASSES):
                 for u in range(HALVES):
@@ -83,48 +76,64 @@ def tile_npertokenswishglu_basis_pb_s_kernel(tc, h, w_down_mix, out):
                     nc.tensor.transpose(
                         hT[:, g, u, :], h_words[:, l, first : first + P], ident_f32[:]
                     )
-            nc.scalar.copy(
-                out=h_grouped[:, l].bitcast(F32), in_=hT[:].rearrange("p g u b -> p g b u")
+            grouped_words = h_grouped[:, l].bitcast(F32)
+            if l < H_COPIES_ON_VECTOR:
+                nc.vector.tensor_copy(out=grouped_words, in_=hT[:].rearrange("p g u b -> p g b u"))
+            else:
+                nc.scalar.copy(out=grouped_words, in_=hT[:].rearrange("p g u b -> p g b u"))
+
+        def sum_weight_squares(l):
+            wT = wt_psum.tile([P, ROWS, P], BF16)
+            for r in range(ROWS):
+                nc.tensor.transpose(wT[:, r, :], w_sb[:, l, r, :], ident_bf[:])
+            nc.scalar.activation(
+                out=w_squares[:, l], in_=wT[:], func=ACT.Square, accum_out=w_sumsq[:, l : l + 1]
             )
+
+        def weight_rsqrt(l):
+            nc.scalar.activation(
+                out=w_rsqrt[:, l : l + 1], in_=w_sumsq[:, l : l + 1], func=ACT.Abs_reciprocal_sqrt
+            )
+
+        def spread_weight_rsqrt(l):
+            w_rsqrt_spread[l] = scale_psum.tile([P, D], F32, name="w_rsqrt_spread")
+            nc.tensor.transpose(
+                w_rsqrt_spread[l][:], w_rsqrt[:, l : l + 1].to_broadcast([P, P]), ident_f32[:]
+            )
+
+        def scale_weight(l):
+            for g in range(PASSES):
+                nc.vector.scalar_tensor_tensor(
+                    out=nd_grouped[:, l, g],
+                    in0=w_rsqrt_spread[l][:].unsqueeze(2).to_broadcast([P, D, PACK]),
+                    scalar=1.0 / EPS,
+                    in1=w_sb[:, l, g * PACK : (g + 1) * PACK, :].rearrange("p t j -> p j t"),
+                    op0=ALU.min,
+                    op1=ALU.mult,
+                )
+
+        def quantise_h(l):
             nc.vector.quantize_mx(
                 out=h_codes[:, l].rearrange("p g b -> p (g b)").bitcast(FP8X4),
                 scales=h_scales[:, l].rearrange("p g b -> p (g b)"),
                 in_=h_grouped[:, l].rearrange("p g b t -> p (g b t)"),
             )
 
-        def spread_scales(first):
-            ls = slice(first, first + PAIR)
-            nc.vector.tensor_scalar_max(
-                out=w_sumsq_floor[:, ls], in0=w_sumsq[:, ls], scalar1=EPS * EPS
-            )
-            nc.vector.reciprocal(out=w_inv_sumsq[:, ls], in_=w_sumsq_floor[:, ls])
-            nc.scalar.activation(
-                out=w_scale_rep[:, ls, :],
-                in_=w_inv_sumsq[:, ls].unsqueeze(2).to_broadcast([P, PAIR, P]),
-                func=ACT.Sqrt,
-            )
-            w_scale = scale_psum.tile([P, PAIR, D], F32)
-            for i in range(PAIR):
-                nc.tensor.transpose(w_scale[:, i, :], w_scale_rep[:, first + i, :], ident_f32[:])
-            return w_scale
-
-        def quantise_nd(l, w_scale_l):
-            nc.vector.tensor_tensor(
-                out=nd_grouped[:, l],
-                in0=w_sb[:, l].rearrange("p (g t) j -> p g j t", t=PACK),
-                in1=w_scale_l.unsqueeze(1).unsqueeze(3).to_broadcast([P, PASSES, D, PACK]),
-                op=ALU.mult,
-            )
+        def quantise_nd(l):
             nc.vector.quantize_mx(
                 out=nd_codes[:, l].rearrange("p g j -> p (g j)").bitcast(FP8X4),
                 scales=nd_scales[:, l].rearrange("p g j -> p (g j)"),
                 in_=nd_grouped[:, l].rearrange("p g j t -> p (g j t)"),
             )
 
-        def multiply(l, y):
+        def multiply(l):
+            if l % BANK_TOKENS == 0:
+                y_bank = y_psum.tile([P, BANK_TOKENS, D], F32)
+                for i in range(BANK_TOKENS):
+                    y[l + i] = y_bank[:, i, :]
             for g in range(PASSES):
                 nc.tensor.matmul_mx(
-                    out=y[:, l % BANK_TOKENS, :],
+                    out=y[l],
                     lhsT=h_codes[:, l, g, :].bitcast(FP8X4),
                     lhsT_scale=h_scales[:, l, g, :],
                     rhs=nd_codes[:, l, g, :].bitcast(FP8X4),
@@ -132,42 +141,43 @@ def tile_npertokenswishglu_basis_pb_s_kernel(tc, h, w_down_mix, out):
                     start=(g == 0),
                     stop=(g == PASSES - 1),
                 )
+
+        def sum_row_squares(l):
             nc.scalar.activation(
-                out=y_squares[:, l, :],
-                in_=y[:, l % BANK_TOKENS, :],
-                func=ACT.Square,
-                accum_out=y_sumsq[:, l : l + 1],
+                out=y_squares[:, l, :], in_=y[l], func=ACT.Square, accum_out=y_sumsq[:, l : l + 1]
             )
 
-        def normalise_and_store(first, y):
-            ls = slice(first, first + BANK_TOKENS)
-            nc.vector.tensor_scalar_max(
-                out=y_sumsq_floor[:, ls], in0=y_sumsq[:, ls], scalar1=EPS * EPS
+        def row_rsqrt(l):
+            nc.scalar.activation(
+                out=y_rsqrt[:, l : l + 1], in_=y_sumsq[:, l : l + 1], func=ACT.Abs_reciprocal_sqrt
             )
-            nc.vector.reciprocal(out=y_inv_sumsq[:, ls], in_=y_sumsq_floor[:, ls])
-            nc.scalar.activation(out=y_scale[:, ls], in_=y_inv_sumsq[:, ls], func=ACT.Sqrt)
-            nc.vector.tensor_tensor(
-                out=out_sb[:, ls, :],
-                in0=y[:],
-                in1=y_scale[:, ls].unsqueeze(2).to_broadcast([P, BANK_TOKENS, D]),
-                op=ALU.mult,
-            )
-            nc.sync.dma_start(out=out[:, ls, :], in_=out_sb[:, ls, :])
 
-        y = None
-        for first in range(0, L + PAIR, PAIR):
-            if first < L:
-                for l in range(first, first + PAIR):
-                    weight_norm(l)
-                    quantise_h(l)
-            if first >= PAIR:
-                done = first - PAIR
-                w_scale = spread_scales(done)
-                if done % BANK_TOKENS == 0:
-                    y = y_psum.tile([P, BANK_TOKENS, D], F32)
-                for i in range(PAIR):
-                    quantise_nd(done + i, w_scale[:, i, :])
-                for i in range(PAIR):
-                    multiply(done + i, y)
-                if (done + PAIR) % BANK_TOKENS == 0:
-                    normalise_and_store(done + PAIR - BANK_TOKENS, y)
+        def normalise_and_store(l):
+            nc.vector.scalar_tensor_tensor(
+                out=out_sb[:, l, :],
+                in0=y_rsqrt[:, l : l + 1].to_broadcast([P, D]),
+                scalar=1.0 / EPS,
+                in1=y[l],
+                op0=ALU.min,
+                op1=ALU.mult,
+            )
+            if l % STORE_TOKENS == STORE_TOKENS - 1:
+                ls = slice(l + 1 - STORE_TOKENS, l + 1)
+                nc.sync.dma_start(out=out[:, ls, :], in_=out_sb[:, ls, :])
+
+        def when_in_range(stage, l):
+            if 0 <= l < L:
+                stage(l)
+
+        for step in range(L + 8):
+            when_in_range(spread_weight_rsqrt, step - 2)
+            when_in_range(sum_weight_squares, step)
+            when_in_range(transpose_h, step)
+            when_in_range(weight_rsqrt, step)
+            when_in_range(row_rsqrt, step - 6)
+            when_in_range(scale_weight, step - 2)
+            when_in_range(quantise_h, step - 1)
+            when_in_range(quantise_nd, step - 2)
+            when_in_range(multiply, step - 3)
+            when_in_range(sum_row_squares, step - 5)
+            when_in_range(normalise_and_store, step - 8)

@@ -22,6 +22,7 @@ FLOPS = 2 * B * L * F * D
 H_COPIES_ON_VECTOR = 2
 STORE_TOKENS = 2
 BANK_TOKENS = 4
+RUN = 4
 
 
 def tile_npertokenswishglu_basis_pb_s_kernel(tc, h, w_down_mix, out):
@@ -52,7 +53,7 @@ def tile_npertokenswishglu_basis_pb_s_kernel(tc, h, w_down_mix, out):
         nc.scalar.activation(out=warm[:], in_=one[:], func=ACT.Abs_reciprocal_sqrt)
 
         w_squares = keep.tile([P, L, ROWS, P], BF16)
-        w_sumsq = keep.tile([P, L], F32)
+        w_sumsq = keep.tile([P, L, ROWS // RUN], F32)
         w_rsqrt = keep.tile([P, L], F32)
         nd_grouped = keep.tile([P, L, PASSES, D, PACK], BF16, align_bytes=64)
         nd_codes = keep.tile([P, L, PASSES, D], U32, align_bytes=64)
@@ -83,16 +84,23 @@ def tile_npertokenswishglu_basis_pb_s_kernel(tc, h, w_down_mix, out):
                 nc.scalar.copy(out=grouped_words, in_=hT[:].rearrange("p g u b -> p g b u"))
 
         def sum_weight_squares(l):
-            wT = wt_psum.tile([P, ROWS, P], BF16)
-            for r in range(ROWS):
-                nc.tensor.transpose(wT[:, r, :], w_sb[:, l, r, :], ident_bf[:])
-            nc.scalar.activation(
-                out=w_squares[:, l], in_=wT[:], func=ACT.Square, accum_out=w_sumsq[:, l : l + 1]
-            )
+            for run in range(ROWS // RUN):
+                wT = wt_psum.tile([P, RUN, P], BF16)
+                for i in range(RUN):
+                    nc.tensor.transpose(wT[:, i, :], w_sb[:, l, run * RUN + i, :], ident_bf[:])
+                nc.scalar.activation(
+                    out=w_squares[:, l, run * RUN : (run + 1) * RUN],
+                    in_=wT[:],
+                    func=ACT.Square,
+                    accum_out=w_sumsq[:, l, run : run + 1],
+                )
 
         def weight_rsqrt(l):
             nc.scalar.activation(
-                out=w_rsqrt[:, l : l + 1], in_=w_sumsq[:, l : l + 1], func=ACT.Abs_reciprocal_sqrt
+                out=w_rsqrt[:, l : l + 1],
+                in_=w_sumsq[:, l, 0:1],
+                func=ACT.Abs_reciprocal_sqrt,
+                bias=w_sumsq[:, l, 1:2],
             )
 
         def spread_weight_rsqrt(l):

@@ -20,8 +20,8 @@ EPS = 1e-12
 FLOPS = 2 * B * L * F * D
 
 H_COPIES_ON_VECTOR = 2
-STORE_TOKENS = 2
 BANK_TOKENS = 4
+PAIR = 2
 RUN = 4
 
 
@@ -66,7 +66,7 @@ def tile_npertokenswishglu_basis_pb_s_kernel(tc, h, w_down_mix, out):
         y_rsqrt = keep.tile([P, L], F32)
         out_sb = keep.tile([P, L, D], F32)
         w_rsqrt_spread = {}
-        y = {}
+        y_banks = {}
 
 
         def transpose_h(l):
@@ -136,12 +136,10 @@ def tile_npertokenswishglu_basis_pb_s_kernel(tc, h, w_down_mix, out):
 
         def multiply(l):
             if l % BANK_TOKENS == 0:
-                y_bank = y_psum.tile([P, BANK_TOKENS, D], F32)
-                for i in range(BANK_TOKENS):
-                    y[l + i] = y_bank[:, i, :]
+                y_banks[l // BANK_TOKENS] = y_psum.tile([P, BANK_TOKENS, D], F32, name="y_bank")
             for g in range(PASSES):
                 nc.tensor.matmul_mx(
-                    out=y[l],
+                    out=y_banks[l // BANK_TOKENS][:, l % BANK_TOKENS, :],
                     lhsT=h_codes[:, l, g, :].bitcast(FP8X4),
                     lhsT_scale=h_scales[:, l, g, :],
                     rhs=nd_codes[:, l, g, :].bitcast(FP8X4),
@@ -152,40 +150,57 @@ def tile_npertokenswishglu_basis_pb_s_kernel(tc, h, w_down_mix, out):
 
         def sum_row_squares(l):
             nc.scalar.activation(
-                out=y_squares[:, l, :], in_=y[l], func=ACT.Square, accum_out=y_sumsq[:, l : l + 1]
+                out=y_squares[:, l, :],
+                in_=y_banks[l // BANK_TOKENS][:, l % BANK_TOKENS, :],
+                func=ACT.Square,
+                accum_out=y_sumsq[:, l : l + 1],
             )
 
-        def row_rsqrt(l):
+        def row_rsqrt(ls):
             nc.scalar.activation(
-                out=y_rsqrt[:, l : l + 1], in_=y_sumsq[:, l : l + 1], func=ACT.Abs_reciprocal_sqrt
+                out=y_rsqrt[:, ls], in_=y_sumsq[:, ls], func=ACT.Abs_reciprocal_sqrt
             )
 
-        def normalise_and_store(l):
+        def normalise_and_store(first):
+            ls = slice(first, first + PAIR)
+            in_bank = first % BANK_TOKENS
             nc.vector.scalar_tensor_tensor(
-                out=out_sb[:, l, :],
-                in0=y_rsqrt[:, l : l + 1].to_broadcast([P, D]),
+                out=out_sb[:, ls, :],
+                in0=y_rsqrt[:, ls].unsqueeze(2).to_broadcast([P, PAIR, D]),
                 scalar=1.0 / EPS,
-                in1=y[l],
+                in1=y_banks[first // BANK_TOKENS][:, in_bank : in_bank + PAIR, :],
                 op0=ALU.min,
                 op1=ALU.mult,
             )
-            if l % STORE_TOKENS == STORE_TOKENS - 1:
-                ls = slice(l + 1 - STORE_TOKENS, l + 1)
-                nc.sync.dma_start(out=out[:, ls, :], in_=out_sb[:, ls, :])
+            nc.sync.dma_start(out=out[:, ls, :], in_=out_sb[:, ls, :])
 
         def when_in_range(stage, l):
             if 0 <= l < L:
                 stage(l)
 
-        for step in range(L + 8):
+        def when_pair_complete(stage, l):
+            if 0 <= l < L and l % PAIR == PAIR - 1:
+                stage(l)
+
+        def multiply_pair(l):
+            multiply(l - 1)
+            multiply(l)
+
+        def row_rsqrt_pair(l):
+            row_rsqrt(slice(l - 1, l + 1))
+
+        def normalise_and_store_pair(l):
+            normalise_and_store(l - 1)
+
+        for step in range(L + 9):
             when_in_range(spread_weight_rsqrt, step - 2)
             when_in_range(sum_weight_squares, step)
             when_in_range(transpose_h, step)
             when_in_range(weight_rsqrt, step)
-            when_in_range(row_rsqrt, step - 6)
+            when_pair_complete(row_rsqrt_pair, step - 6)
             when_in_range(scale_weight, step - 2)
             when_in_range(quantise_h, step - 1)
             when_in_range(quantise_nd, step - 2)
-            when_in_range(multiply, step - 3)
+            when_pair_complete(multiply_pair, step - 4)
             when_in_range(sum_row_squares, step - 5)
-            when_in_range(normalise_and_store, step - 8)
+            when_pair_complete(normalise_and_store_pair, step - 8)

@@ -35,10 +35,15 @@ def tile_npertokenswishglu_basis_pb_s_kernel(tc, h, w_down_mix, out):
         w_sb = keep.tile([P, L, ROWS, D], BF16)
         h_sb = keep.tile([P, L, F], BF16)
         for l in range(L):
-            nc.sync.dma_start(
-                out=w_sb[:, l].rearrange("p (s e) j -> p s (e j)", e=2),
-                in_=w_down_mix[l].rearrange("(s p e) j -> p s (e j)", p=P, e=2),
-            )
+            for run in range(ROWS // RUN):
+                nc.sync.dma_start(
+                    out=w_sb[:, l, run * RUN : (run + 1) * RUN].rearrange(
+                        "p (u e) j -> p u (e j)", e=2
+                    ),
+                    in_=w_down_mix[l, run * RUN * P : (run + 1) * RUN * P, :].rearrange(
+                        "(u p e) j -> p u (e j)", p=P, e=2
+                    ),
+                )
             nc.sync.dma_start(out=h_sb[:, l, :], in_=h[:, l, :])
         h_words = h_sb[:].bitcast(F32)
 

import concourse.mybir as mybir
from concourse.masks import make_identity

F32 = mybir.dt.float32
BF16 = mybir.dt.bfloat16
U32 = mybir.dt.uint32
U8 = mybir.dt.uint8
FP8X4 = mybir.dt.float8_e4m3fn_x4
ACT = mybir.ActivationFunctionType
ALU = mybir.AluOpType

P = 128
B, L, F, D = 128, 8, 1024, 128
PACK = 4
PASSES = F // (P * PACK)
ROWS = F // P
HALVES = 2
EPS = 1e-12

FLOPS = 2 * B * L * F * D

H_COPIES_ON_VECTOR = 2
BANK_TOKENS = 4
PAIR = 2
RUN = 4


def tile_npertokenswishglu_basis_pb_s_kernel(tc, h, w_down_mix, out):
    nc = tc.nc
    with tc.tile_pool(name="keep", bufs=1) as keep, tc.psum_pool(
        name="wt_psum", bufs=2
    ) as wt_psum, tc.psum_pool(name="ht_psum", bufs=2) as ht_psum, tc.psum_pool(
        name="scale_psum", bufs=2
    ) as scale_psum, tc.psum_pool(name="y_psum", bufs=2) as y_psum, tc.manual_schedule():
        w_sb = keep.tile([P, L, ROWS, D], BF16)
        h_sb = keep.tile([P, L, F], BF16)
        for l in range(L):
            for run in range(ROWS // RUN):
                nc.sync.dma_start(
                    out=w_sb[:, l, run * RUN : (run + 1) * RUN].rearrange(
                        "p (u e) j -> p u (e j)", e=2
                    ),
                    in_=w_down_mix[l, run * RUN * P : (run + 1) * RUN * P, :].rearrange(
                        "(u p e) j -> p u (e j)", p=P, e=2
                    ),
                )
            nc.sync.dma_start(out=h_sb[:, l, :], in_=h[:, l, :])
        h_words = h_sb[:].bitcast(F32)

        ident_bf = keep.tile([P, P], BF16)
        make_identity(nc, ident_bf[:])
        ident_f32 = keep.tile([P, P], F32)
        make_identity(nc, ident_f32[:])

        one = keep.tile([P, 1], F32)
        nc.vector.memset(one[:], 1.0)
        warm = keep.tile([P, 1], F32)
        nc.scalar.activation(out=warm[:], in_=one[:], func=ACT.Abs_reciprocal_sqrt)

        w_squares = keep.tile([P, L, ROWS, P], BF16)
        w_sumsq = keep.tile([P, L, ROWS // RUN], F32)
        w_rsqrt = keep.tile([P, L], F32)
        nd_grouped = keep.tile([P, L, PASSES, D, PACK], BF16, align_bytes=64)
        nd_codes = keep.tile([P, L, PASSES, D], U32, align_bytes=64)
        nd_scales = keep.tile([P, L, PASSES, D], U8, align_bytes=64)
        h_grouped = keep.tile([P, L, PASSES, B, PACK], BF16, align_bytes=64)
        h_codes = keep.tile([P, L, PASSES, B], U32, align_bytes=64)
        h_scales = keep.tile([P, L, PASSES, B], U8, align_bytes=64)
        y_squares = keep.tile([P, L, D], F32)
        y_sumsq = keep.tile([P, L], F32)
        y_rsqrt = keep.tile([P, L], F32)
        out_sb = keep.tile([P, L, D], F32)
        w_rsqrt_spread = {}
        y_banks = {}


        def transpose_h(l):
            hT = ht_psum.tile([P, PASSES, HALVES, B], F32)
            for g in range(PASSES):
                for u in range(HALVES):
                    first = (g * HALVES + u) * P
                    nc.tensor.transpose(
                        hT[:, g, u, :], h_words[:, l, first : first + P], ident_f32[:]
                    )
            grouped_words = h_grouped[:, l].bitcast(F32)
            if l < H_COPIES_ON_VECTOR:
                nc.vector.tensor_copy(out=grouped_words, in_=hT[:].rearrange("p g u b -> p g b u"))
            else:
                nc.scalar.copy(out=grouped_words, in_=hT[:].rearrange("p g u b -> p g b u"))

        def sum_weight_squares(l):
            for run in range(ROWS // RUN):
                wT = wt_psum.tile([P, RUN, P], BF16)
                for i in range(RUN):
                    nc.tensor.transpose(wT[:, i, :], w_sb[:, l, run * RUN + i, :], ident_bf[:])
                nc.scalar.activation(
                    out=w_squares[:, l, run * RUN : (run + 1) * RUN],
                    in_=wT[:],
                    func=ACT.Square,
                    accum_out=w_sumsq[:, l, run : run + 1],
                )

        def weight_rsqrt(l):
            nc.scalar.activation(
                out=w_rsqrt[:, l : l + 1],
                in_=w_sumsq[:, l, 0:1],
                func=ACT.Abs_reciprocal_sqrt,
                bias=w_sumsq[:, l, 1:2],
            )

        def spread_weight_rsqrt(l):
            w_rsqrt_spread[l] = scale_psum.tile([P, D], F32, name="w_rsqrt_spread")
            nc.tensor.transpose(
                w_rsqrt_spread[l][:], w_rsqrt[:, l : l + 1].to_broadcast([P, P]), ident_f32[:]
            )

        def scale_weight(l):
            for g in range(PASSES):
                nc.vector.scalar_tensor_tensor(
                    out=nd_grouped[:, l, g],
                    in0=w_rsqrt_spread[l][:].unsqueeze(2).to_broadcast([P, D, PACK]),
                    scalar=1.0 / EPS,
                    in1=w_sb[:, l, g * PACK : (g + 1) * PACK, :].rearrange("p t j -> p j t"),
                    op0=ALU.min,
                    op1=ALU.mult,
                )

        def quantise_h(l):
            nc.vector.quantize_mx(
                out=h_codes[:, l].rearrange("p g b -> p (g b)").bitcast(FP8X4),
                scales=h_scales[:, l].rearrange("p g b -> p (g b)"),
                in_=h_grouped[:, l].rearrange("p g b t -> p (g b t)"),
            )

        def quantise_nd(l):
            nc.vector.quantize_mx(
                out=nd_codes[:, l].rearrange("p g j -> p (g j)").bitcast(FP8X4),
                scales=nd_scales[:, l].rearrange("p g j -> p (g j)"),
                in_=nd_grouped[:, l].rearrange("p g j t -> p (g j t)"),
            )

        def multiply(l):
            if l % BANK_TOKENS == 0:
                y_banks[l // BANK_TOKENS] = y_psum.tile([P, BANK_TOKENS, D], F32, name="y_bank")
            for g in range(PASSES):
                nc.tensor.matmul_mx(
                    out=y_banks[l // BANK_TOKENS][:, l % BANK_TOKENS, :],
                    lhsT=h_codes[:, l, g, :].bitcast(FP8X4),
                    lhsT_scale=h_scales[:, l, g, :],
                    rhs=nd_codes[:, l, g, :].bitcast(FP8X4),
                    rhs_scale=nd_scales[:, l, g, :],
                    start=(g == 0),
                    stop=(g == PASSES - 1),
                )

        def sum_row_squares(l):
            nc.scalar.activation(
                out=y_squares[:, l, :],
                in_=y_banks[l // BANK_TOKENS][:, l % BANK_TOKENS, :],
                func=ACT.Square,
                accum_out=y_sumsq[:, l : l + 1],
            )

        def row_rsqrt(ls):
            nc.scalar.activation(
                out=y_rsqrt[:, ls], in_=y_sumsq[:, ls], func=ACT.Abs_reciprocal_sqrt
            )

        def normalise_and_store(first):
            ls = slice(first, first + PAIR)
            in_bank = first % BANK_TOKENS
            nc.vector.scalar_tensor_tensor(
                out=out_sb[:, ls, :],
                in0=y_rsqrt[:, ls].unsqueeze(2).to_broadcast([P, PAIR, D]),
                scalar=1.0 / EPS,
                in1=y_banks[first // BANK_TOKENS][:, in_bank : in_bank + PAIR, :],
                op0=ALU.min,
                op1=ALU.mult,
            )
            nc.sync.dma_start(out=out[:, ls, :], in_=out_sb[:, ls, :])

        def when_in_range(stage, l):
            if 0 <= l < L:
                stage(l)

        def when_pair_complete(stage, l):
            if 0 <= l < L and l % PAIR == PAIR - 1:
                stage(l)

        def multiply_pair(l):
            multiply(l - 1)
            multiply(l)

        def row_rsqrt_pair(l):
            row_rsqrt(slice(l - 1, l + 1))

        def normalise_and_store_pair(l):
            normalise_and_store(l - 1)

        for step in range(L + 9):
            when_in_range(spread_weight_rsqrt, step - 2)
            when_in_range(sum_weight_squares, step)
            when_in_range(transpose_h, step)
            when_in_range(weight_rsqrt, step)
            when_pair_complete(row_rsqrt_pair, step - 6)
            when_in_range(scale_weight, step - 2)
            when_in_range(quantise_h, step - 1)
            when_in_range(quantise_nd, step - 2)
            when_pair_complete(multiply_pair, step - 4)
            when_in_range(sum_row_squares, step - 5)
            when_pair_complete(normalise_and_store_pair, step - 8)
